import numpy as np
import ml_dtypes


def mxq(x, axis, fmt="e4m3"):
    dtype, down = {"e4m3": (ml_dtypes.float8_e4m3fn, 7), "e5m2": (ml_dtypes.float8_e5m2, 14)}[fmt]
    v = np.moveaxis(np.asarray(x, np.float32).astype(ml_dtypes.bfloat16).astype(np.float64), axis, -1)
    blocks = v.reshape(v.shape[:-1] + (-1, 32))
    amax = np.abs(blocks).max(-1, keepdims=True)
    byte = np.maximum(np.where(amax > 0, np.frexp(amax)[1] - 1 + 127, 0) - down, 1)
    scale = np.exp2(byte - 127.0)
    codes = (blocks / scale).astype(np.float32).astype(dtype).astype(np.float64)
    return np.moveaxis((codes * scale).reshape(v.shape), -1, axis)


WIDE = False


def mx_kscale(k):
    if not WIDE:
        return np.ones(k)
    levels = np.array([10, -10, 5, -5, 0])
    if k % 512:
        return np.exp2(np.random.permutation(np.resize(levels, k // 32))).repeat(32)
    a = np.empty((k // 512, 16))
    for p in range(k // 512):
        a[p, :8] = np.random.permutation(np.resize(levels, 8))
        for g in range(8):
            far = levels[np.abs(levels - a[p, g]) >= 10]
            a[p, g + 8] = far[np.random.randint(len(far))]
    return np.exp2(a.ravel()).repeat(32)


BF16 = ml_dtypes.bfloat16


def bf(x):
    return np.asarray(x, np.float32).astype(BF16)


def f64(x):
    return np.asarray(x).astype(np.float64)


B, IN, H, NS, SS, CS, NA = 128, 256, 1024, 4, 8, 128, 3
NC = NS * CS


def setup_inputs():
    s = mx_kscale(H)
    return {
        "h": bf(np.tanh(np.random.standard_normal((B, H))) * s),
        "act_logits": bf(np.random.standard_normal((B, NS * NA)) * 1.5),
        "stacks": bf(np.random.standard_normal((B, NS, SS, CS)) * 1.5),
        "W_push": bf(np.random.standard_normal((NC, H)) * 5.0 / np.sqrt(H) / s),
        "b_push": bf(np.random.standard_normal(NC) * 0.7),
    }


def reference(h, act_logits, stacks, W_push, b_push):
    st = f64(stacks)
    push = ((mxq(f64(h), 1, "e4m3") @ mxq(f64(W_push), 1, "e4m3").T) + f64(b_push)).reshape(B, NS, CS)
    lg = f64(act_logits)
    e = np.exp(lg - lg.max(-1, keepdims=True))
    act = (e / e.sum(-1, keepdims=True)).reshape(B, NS, NA)
    pa, po, no = act[..., 0][..., None], act[..., 1][..., None], act[..., 2][..., None]
    top_new = pa * push + po * st[:, :, 1, :] + no * st[:, :, 0, :]
    zeros_tail = np.zeros((B, NS, 1, CS))
    pop_rest = np.concatenate([st[:, :, 2:, :], zeros_tail], axis=2)
    rest = (pa[:, :, :, None] * st[:, :, :-1, :]
            + po[:, :, :, None] * pop_rest
            + no[:, :, :, None] * st[:, :, 1:, :])
    return np.concatenate([top_new[:, :, None, :], rest], axis=2)

@@ -1,0 +1,187 @@
+from contextlib import ExitStack
+
+import concourse.mybir as mybir
+from concourse.masks import make_identity
+
+F32 = mybir.dt.float32
+BF16 = mybir.dt.bfloat16
+U32 = mybir.dt.uint32
+U8 = mybir.dt.uint8
+FP8X4 = mybir.dt.float8_e4m3fn_x4
+ACT = mybir.ActivationFunctionType
+ALU = mybir.AluOpType
+AX = mybir.AxisListType
+
+P = 128
+H = 1024
+NS = 4
+SS = 8
+HALF = SS // 2
+CS = 128
+NA = 3
+PACK = 4
+K_PASS = P * PACK
+PASSES = H // K_PASS
+PAIRS = 2
+
+FLOPS = 2 * P * H * NS * CS
+
+
+def tile_stackrnncore_pa_s_kernel(tc, h, act_logits, stacks, W_push, b_push, out):
+    nc = tc.nc
+    with ExitStack() as ctx:
+        keep = ctx.enter_context(tc.tile_pool(name="keep", bufs=1))
+        psum = ctx.enter_context(tc.psum_pool(name="psum", bufs=1))
+        ctx.enter_context(tc.manual_schedule())
+
+        logits = keep.tile([P, NS * NA], BF16)
+        nc.sync.dma_start(out=logits[:], in_=act_logits)
+
+        old = keep.tile([P, NS, SS, CS], BF16)
+        h_rows = keep.tile([P, H], BF16)
+        w_rows = [keep.tile([P, H], BF16, name="w_rows%d" % n) for n in range(NS)]
+        nc.sync.dma_start(out=old[:, 0], in_=stacks[:, 0])
+        nc.sync.dma_start(out=old[:, 1], in_=stacks[:, 1])
+        nc.sync.dma_start(out=h_rows[:], in_=h)
+        for n in range(NS):
+            nc.sync.dma_start(out=w_rows[n][:], in_=W_push[n * CS : (n + 1) * CS, :])
+        nc.sync.dma_start(out=old[:, 2], in_=stacks[:, 2])
+        nc.sync.dma_start(out=old[:, 3], in_=stacks[:, 3])
+        bias_col = keep.tile([P, NS], BF16)
+        with nc.allow_non_contiguous_dma(reason="512 single elements, once, behind all else"):
+            nc.sync.dma_start(out=bias_col[:], in_=b_push.rearrange("(n c) -> c n", c=CS))
+
+        identity = keep.tile([P, P], F32)
+        make_identity(nc, identity[:])
+
+        zero = keep.tile([P, 1], F32)
+        nc.vector.memset(zero[:], 0.0)
+        one = keep.tile([P, 1], F32)
+        nc.scalar.activation(out=one[:], in_=zero[:], func=ACT.Exp)
+
+        neg_max = keep.tile([P, 1], F32)
+        nc.vector.reduce_max(out=neg_max[:], in_=logits[:], axis=AX.X, negate=True)
+        expd = keep.tile([P, NS * NA], F32)
+        exp_sum = keep.tile([P, 1], F32)
+        nc.scalar.activation(
+            out=expd[:], in_=logits[:], func=ACT.Exp, bias=neg_max[:], accum_out=exp_sum[:]
+        )
+        inv_sum = keep.tile([P, 1], F32)
+        nc.vector.reciprocal(out=inv_sum[:], in_=exp_sum[:])
+        act = keep.tile([P, NS, NA], F32)
+        nc.vector.tensor_scalar_mul(
+            out=act[:].rearrange("p n a -> p (n a)"), in0=expd[:], scalar1=inv_sum[:]
+        )
+
+        new = keep.tile([P, NS, SS, CS], F32)
+
+        nc.vector.tensor_scalar(
+            out=new[:, 0, 0:HALF],
+            in0=old[:, 0, 0:HALF],
+            scalar1=expd[:, 2:3],
+            scalar2=inv_sum[:],
+            op0=ALU.mult,
+            op1=ALU.mult,
+        )
+
+        def keep_term(n, first):
+            nc.scalar.activation(
+                out=new[:, n, first : first + HALF],
+                in_=old[:, n, first : first + HALF],
+                func=ACT.Copy,
+                scale=act[:, n, 2:3],
+            )
+
+        def add_term(n, first, last, shift, action):
+            nc.vector.scalar_tensor_tensor(
+                out=new[:, n, first:last],
+                in0=old[:, n, first + shift : last + shift],
+                scalar=act[:, n, action : action + 1],
+                in1=new[:, n, first:last],
+                op0=ALU.mult,
+                op1=ALU.add,
+            )
+
+        def neighbour_terms(n):
+            add_term(n, 1, HALF, -1, 0)
+            add_term(n, HALF, SS, -1, 0)
+            add_term(n, 0, HALF, 1, 1)
+            nc.sync.dma_start(out=out[:, n, 1:HALF, :], in_=new[:, n, 1:HALF, :])
+            add_term(n, HALF, SS - 1, 1, 1)
+            nc.sync.dma_start(out=out[:, n, HALF:SS, :], in_=new[:, n, HALF:SS, :])
+
+        keep_term(0, HALF)
+        keep_term(1, 0)
+        keep_term(1, HALF)
+        neighbour_terms(0)
+        neighbour_terms(1)
+
+        def regroup(rows, name):
+            bank = psum.tile([P, PASSES, PAIRS, P], F32, name="bank_" + name)
+            words = rows.bitcast(F32)
+            for g in range(PASSES):
+                for u in range(PAIRS):
+                    first = g * PAIRS * P + u
+                    nc.tensor.transpose(
+                        bank[:, g, u, :], words[:, first : (g + 1) * PAIRS * P : PAIRS], identity[:]
+                    )
+            grouped = keep.tile([P, PASSES * P * PACK], BF16, align_bytes=64, name="grouped_" + name)
+            nc.scalar.copy(
+                out=grouped[:].bitcast(F32).rearrange("p (g r u) -> p g r u", g=PASSES, u=PAIRS),
+                in_=bank[:].rearrange("p g u r -> p g r u"),
+            )
+            return grouped
+
+        def quantise(grouped, name):
+            codes = keep.tile([P, PASSES, P], U32, align_bytes=64, name="codes_" + name)
+            scales = keep.tile([P, PASSES, P], U8, align_bytes=64, name="scales_" + name)
+            nc.vector.quantize_mx(
+                out=codes[:].rearrange("p g r -> p (g r)").bitcast(FP8X4),
+                scales=scales[:].rearrange("p g r -> p (g r)"),
+                in_=grouped[:],
+            )
+            return codes, scales
+
+        h_grouped = regroup(h_rows[:], "h")
+        w_grouped = [regroup(w_rows[n][:], "w%d" % n) for n in range(NS)]
+        h_codes, h_scales = quantise(h_grouped, "h")
+        w_quantised = [quantise(w_grouped[n], "w%d" % n) for n in range(NS)]
+
+        push_t = psum.tile([P, NS, P], F32)
+        for n in range(NS):
+            w_codes, w_scales = w_quantised[n]
+            for g in range(PASSES):
+                nc.tensor.matmul_mx(
+                    out=push_t[:, n, :],
+                    lhsT=w_codes[:, g, :].bitcast(FP8X4),
+                    lhsT_scale=w_scales[:, g, :],
+                    rhs=h_codes[:, g, :].bitcast(FP8X4),
+                    rhs_scale=h_scales[:, g, :],
+                    start=(g == 0),
+                    stop=(g == PASSES - 1),
+                )
+
+        for n in (2, 3):
+            keep_term(n, 0)
+            keep_term(n, HALF)
+        neighbour_terms(2)
+        neighbour_terms(3)
+
+        biased_t = keep.tile([P, NS, P], F32)
+        biased = psum.tile([P, NS, CS], F32)
+        for n in range(NS):
+            nc.scalar.activation(
+                out=biased_t[:, n, :], in_=push_t[:, n, :], func=ACT.Identity, bias=bias_col[:, n : n + 1]
+            )
+        for n in range(NS):
+            nc.tensor.transpose(biased[:, n, :], biased_t[:, n, :], identity[:])
+        for n in range(NS):
+            nc.vector.scalar_tensor_tensor(
+                out=new[:, n, 0, :],
+                in0=biased[:, n, :],
+                scalar=act[:, n, 0:1],
+                in1=new[:, n, 0, :],
+                op0=ALU.mult,
+                op1=ALU.add,
+            )
+            nc.sync.dma_start(out=out[:, n, 0, :], in_=new[:, n, 0, :])

@@ -84,12 +84,9 @@ def tile_stackrnncore_pa_s_kernel(tc, h, act_logits, stacks, W_push, b_push, out
             op1=ALU.mult,
         )
 
-        def keep_term(n, first):
+        def keep_term(n, first, last):
             nc.scalar.activation(
-                out=new[:, n, first : first + HALF],
-                in_=old[:, n, first : first + HALF],
-                func=ACT.Copy,
-                scale=act[:, n, 2:3],
+                out=new[:, n, first:last], in_=old[:, n, first:last], func=ACT.Copy, scale=act[:, n, 2:3]
             )
 
         def add_term(n, first, last, shift, action):
@@ -102,21 +99,16 @@ def tile_stackrnncore_pa_s_kernel(tc, h, act_logits, stacks, W_push, b_push, out
                 op1=ALU.add,
             )
 
-        def neighbour_terms(n):
-            add_term(n, 1, HALF, -1, 0)
-            add_term(n, HALF, SS, -1, 0)
-            add_term(n, 0, HALF, 1, 1)
-            nc.sync.dma_start(out=out[:, n, 1:HALF, :], in_=new[:, n, 1:HALF, :])
-            add_term(n, HALF, SS - 1, 1, 1)
-            nc.sync.dma_start(out=out[:, n, HALF:SS, :], in_=new[:, n, HALF:SS, :])
+        def push_term(n, first, last):
+            add_term(n, first, last, -1, 0)
 
-        keep_term(0, HALF)
-        keep_term(1, 0)
-        keep_term(1, HALF)
-        neighbour_terms(0)
-        neighbour_terms(1)
+        def pop_term(n, first, last):
+            add_term(n, first, last, 1, 1)
 
-        def regroup(rows, name):
+        def store(n, first, last):
+            nc.sync.dma_start(out=out[:, n, first:last, :], in_=new[:, n, first:last, :])
+
+        def turn(rows, name):
             bank = psum.tile([P, PASSES, PAIRS, P], F32, name="bank_" + name)
             words = rows.bitcast(F32)
             for g in range(PASSES):
@@ -125,6 +117,9 @@ def tile_stackrnncore_pa_s_kernel(tc, h, act_logits, stacks, W_push, b_push, out
                     nc.tensor.transpose(
                         bank[:, g, u, :], words[:, first : (g + 1) * PAIRS * P : PAIRS], identity[:]
                     )
+            return bank
+
+        def regroup(bank, name):
             grouped = keep.tile([P, PASSES * P * PACK], BF16, align_bytes=64, name="grouped_" + name)
             nc.scalar.copy(
                 out=grouped[:].bitcast(F32).rearrange("p (g r u) -> p g r u", g=PASSES, u=PAIRS),
@@ -142,10 +137,34 @@ def tile_stackrnncore_pa_s_kernel(tc, h, act_logits, stacks, W_push, b_push, out
             )
             return codes, scales
 
-        h_grouped = regroup(h_rows[:], "h")
-        w_grouped = [regroup(w_rows[n][:], "w%d" % n) for n in range(NS)]
+        h_bank = turn(h_rows[:], "h")
+        w_banks = [turn(w_rows[n][:], "w%d" % n) for n in range(NS)]
+
+        keep_term(0, HALF, SS)
+        keep_term(1, 0, SS)
+        h_grouped = regroup(h_bank, "h")
+        w_grouped = [regroup(w_banks[0], "w0"), regroup(w_banks[1], "w1")]
+        keep_term(2, 0, SS)
+        w_grouped += [regroup(w_banks[2], "w2"), regroup(w_banks[3], "w3")]
+        keep_term(3, 0, SS)
+
+        push_term(0, 1, HALF)
+        push_term(0, HALF, SS)
+        pop_term(0, 0, HALF)
+        store(0, 1, HALF)
+        pop_term(0, HALF, SS - 1)
+        store(0, HALF, SS)
+        push_term(1, 1, SS)
         h_codes, h_scales = quantise(h_grouped, "h")
-        w_quantised = [quantise(w_grouped[n], "w%d" % n) for n in range(NS)]
+        pop_term(1, 0, SS - 1)
+        store(1, 1, SS)
+        w_quantised = [quantise(w_grouped[0], "w0")]
+        w_quantised.append(quantise(w_grouped[1], "w1"))
+        push_term(2, 1, SS)
+        w_quantised.append(quantise(w_grouped[2], "w2"))
+        w_quantised.append(quantise(w_grouped[3], "w3"))
+        pop_term(2, 0, SS - 1)
+        store(2, 1, SS)
 
         push_t = psum.tile([P, NS, P], F32)
         for n in range(NS):
@@ -161,12 +180,6 @@ def tile_stackrnncore_pa_s_kernel(tc, h, act_logits, stacks, W_push, b_push, out
                     stop=(g == PASSES - 1),
                 )
 
-        for n in (2, 3):
-            keep_term(n, 0)
-            keep_term(n, HALF)
-        neighbour_terms(2)
-        neighbour_terms(3)
-
         biased_t = keep.tile([P, NS, P], F32)
         biased = psum.tile([P, NS, CS], F32)
         for n in range(NS):
@@ -175,7 +188,8 @@ def tile_stackrnncore_pa_s_kernel(tc, h, act_logits, stacks, W_push, b_push, out
             )
         for n in range(NS):
             nc.tensor.transpose(biased[:, n, :], biased_t[:, n, :], identity[:])
-        for n in range(NS):
+
+        def top_cell(n):
             nc.vector.scalar_tensor_tensor(
                 out=new[:, n, 0, :],
                 in0=biased[:, n, :],
@@ -184,4 +198,19 @@ def tile_stackrnncore_pa_s_kernel(tc, h, act_logits, stacks, W_push, b_push, out
                 op0=ALU.mult,
                 op1=ALU.add,
             )
-            nc.sync.dma_start(out=out[:, n, 0, :], in_=new[:, n, 0, :])
+
+        push_term(3, 1, HALF)
+        push_term(3, HALF, SS)
+        pop_term(3, 0, HALF)
+        top_cell(0)
+        store(0, 0, 1)
+        top_cell(1)
+        store(1, 0, 1)
+        top_cell(2)
+        store(2, 0, 1)
+        top_cell(3)
+        store(3, 0, HALF)
+        pop_term(3, HALF, SS - 2)
+        store(3, HALF, SS - 2)
+        pop_term(3, SS - 2, SS - 1)
+        store(3, SS - 2, SS)

@@ -42,10 +42,10 @@ def tile_stackrnncore_pa_s_kernel(tc, h, act_logits, stacks, W_push, b_push, out
         w_rows = [keep.tile([P, H], BF16, name="w_rows%d" % n) for n in range(NS)]
         nc.sync.dma_start(out=old[:, 0], in_=stacks[:, 0])
         nc.sync.dma_start(out=old[:, 1], in_=stacks[:, 1])
+        nc.sync.dma_start(out=old[:, 2], in_=stacks[:, 2])
         nc.sync.dma_start(out=h_rows[:], in_=h)
         for n in range(NS):
             nc.sync.dma_start(out=w_rows[n][:], in_=W_push[n * CS : (n + 1) * CS, :])
-        nc.sync.dma_start(out=old[:, 2], in_=stacks[:, 2])
         nc.sync.dma_start(out=old[:, 3], in_=stacks[:, 3])
         bias_col = keep.tile([P, NS], BF16)
         with nc.allow_non_contiguous_dma(reason="512 single elements, once, behind all else"):
@@ -142,29 +142,25 @@ def tile_stackrnncore_pa_s_kernel(tc, h, act_logits, stacks, W_push, b_push, out
 
         keep_term(0, HALF, SS)
         keep_term(1, 0, SS)
-        h_grouped = regroup(h_bank, "h")
-        w_grouped = [regroup(w_banks[0], "w0"), regroup(w_banks[1], "w1")]
         keep_term(2, 0, SS)
-        w_grouped += [regroup(w_banks[2], "w2"), regroup(w_banks[3], "w3")]
+        h_grouped = regroup(h_bank, "h")
+        w_grouped = [regroup(w_banks[n], "w%d" % n) for n in range(NS)]
         keep_term(3, 0, SS)
 
         push_term(0, 1, HALF)
         push_term(0, HALF, SS)
         pop_term(0, 0, HALF)
         store(0, 1, HALF)
+        push_term(1, 1, SS)
         pop_term(0, HALF, SS - 1)
         store(0, HALF, SS)
-        push_term(1, 1, SS)
-        h_codes, h_scales = quantise(h_grouped, "h")
+        push_term(2, 1, SS)
         pop_term(1, 0, SS - 1)
         store(1, 1, SS)
-        w_quantised = [quantise(w_grouped[0], "w0")]
-        w_quantised.append(quantise(w_grouped[1], "w1"))
-        push_term(2, 1, SS)
-        w_quantised.append(quantise(w_grouped[2], "w2"))
-        w_quantised.append(quantise(w_grouped[3], "w3"))
+        h_codes, h_scales = quantise(h_grouped, "h")
         pop_term(2, 0, SS - 1)
         store(2, 1, SS)
+        w_quantised = [quantise(w_grouped[n], "w%d" % n) for n in range(NS)]
 
         push_t = psum.tile([P, NS, P], F32)
         for n in range(NS):
@@ -202,15 +198,9 @@ def tile_stackrnncore_pa_s_kernel(tc, h, act_logits, stacks, W_push, b_push, out
         push_term(3, 1, HALF)
         push_term(3, HALF, SS)
         pop_term(3, 0, HALF)
-        top_cell(0)
-        store(0, 0, 1)
-        top_cell(1)
-        store(1, 0, 1)
-        top_cell(2)
-        store(2, 0, 1)
-        top_cell(3)
-        store(3, 0, HALF)
-        pop_term(3, HALF, SS - 2)
-        store(3, HALF, SS - 2)
-        pop_term(3, SS - 2, SS - 1)
-        store(3, SS - 2, SS)
+        store(3, 1, HALF)
+        pop_term(3, HALF, SS - 1)
+        store(3, HALF, SS)
+        for n in range(NS):
+            top_cell(n)
+            store(n, 0, 1)

@@ -44,15 +44,17 @@ def tile_stackrnncore_pa_s_kernel(tc, h, act_logits, stacks, W_push, b_push, out
         nc.sync.dma_start(out=old[:, 1], in_=stacks[:, 1])
         nc.sync.dma_start(out=old[:, 2], in_=stacks[:, 2])
         nc.sync.dma_start(out=h_rows[:], in_=h)
+        bias_rows = keep.tile([P, CS], BF16)
+        nc.gpsimd.memset(bias_rows[:], 0.0)
+        nc.sync.dma_start(out=bias_rows[0:NS, :], in_=b_push.rearrange("(n c) -> n c", c=CS))
         for n in range(NS):
             nc.sync.dma_start(out=w_rows[n][:], in_=W_push[n * CS : (n + 1) * CS, :])
         nc.sync.dma_start(out=old[:, 3], in_=stacks[:, 3])
-        bias_col = keep.tile([P, NS], BF16)
-        with nc.allow_non_contiguous_dma(reason="512 single elements, once, behind all else"):
-            nc.sync.dma_start(out=bias_col[:], in_=b_push.rearrange("(n c) -> c n", c=CS))
 
         identity = keep.tile([P, P], F32)
         make_identity(nc, identity[:])
+        identity_bf16 = keep.tile([P, P], BF16)
+        make_identity(nc, identity_bf16[:])
 
         zero = keep.tile([P, 1], F32)
         nc.vector.memset(zero[:], 0.0)
@@ -140,12 +142,17 @@ def tile_stackrnncore_pa_s_kernel(tc, h, act_logits, stacks, W_push, b_push, out
         h_bank = turn(h_rows[:], "h")
         w_banks = [turn(w_rows[n][:], "w%d" % n) for n in range(NS)]
 
+        bias_bank = psum.tile([P, P], BF16)
+        nc.tensor.transpose(bias_bank[:], bias_rows[:], identity_bf16[:])
+
         keep_term(0, HALF, SS)
         keep_term(1, 0, SS)
         keep_term(2, 0, SS)
         h_grouped = regroup(h_bank, "h")
         w_grouped = [regroup(w_banks[n], "w%d" % n) for n in range(NS)]
         keep_term(3, 0, SS)
+        bias_col = keep.tile([P, NS], F32)
+        nc.scalar.copy(out=bias_col[:], in_=bias_bank[:, 0:NS])
 
         push_term(0, 1, HALF)
         push_term(0, HALF, SS)

@@ -16,6 +16,7 @@ P = 128
 H = 1024
 NS = 4
 SS = 8
+LATE = 5
 HALF = SS // 2
 CS = 128
 NA = 3
@@ -142,7 +143,7 @@ def tile_stackrnncore_pa_s_kernel(tc, h, act_logits, stacks, W_push, b_push, out
         h_bank = turn(h_rows[:], "h")
         w_banks = [turn(w_rows[n][:], "w%d" % n) for n in range(NS)]
 
-        bias_bank = psum.tile([P, P], BF16)
+        bias_bank = psum.tile([P, P], BF16, name="bias_bank")
         nc.tensor.transpose(bias_bank[:], bias_rows[:], identity_bf16[:])
 
         keep_term(0, HALF, SS)
@@ -151,6 +152,10 @@ def tile_stackrnncore_pa_s_kernel(tc, h, act_logits, stacks, W_push, b_push, out
         h_grouped = regroup(h_bank, "h")
         w_grouped = [regroup(w_banks[n], "w%d" % n) for n in range(NS)]
         keep_term(3, 0, SS)
+        popped = keep.tile([P, SS - 1 - LATE, CS], F32)
+        nc.scalar.activation(
+            out=popped[:], in_=old[:, 3, LATE + 1 : SS], func=ACT.Copy, scale=act[:, 3, 1:2]
+        )
         bias_col = keep.tile([P, NS], F32)
         nc.scalar.copy(out=bias_col[:], in_=bias_bank[:, 0:NS])
 
@@ -165,16 +170,22 @@ def tile_stackrnncore_pa_s_kernel(tc, h, act_logits, stacks, W_push, b_push, out
         pop_term(1, 0, SS - 1)
         store(1, 1, SS)
         h_codes, h_scales = quantise(h_grouped, "h")
+        w_quantised = [quantise(w_grouped[n], "w%d" % n) for n in range(NS)]
         pop_term(2, 0, SS - 1)
         store(2, 1, SS)
-        w_quantised = [quantise(w_grouped[n], "w%d" % n) for n in range(NS)]
 
-        push_t = psum.tile([P, NS, P], F32)
+        biased_t = keep.tile([P, NS, P], F32)
+        biased = []
+        push_t = []
         for n in range(NS):
+            push_t.append(psum.tile([P, P], F32, name=("bank_push", "bank_h", "bank_w0", "bank_w1")[n]))
+            biased.append(psum.tile([P, CS], F32, name=("bank_top", "bank_w2", "bank_w3", "bias_bank")[n]))
+
+        def multiply(n):
             w_codes, w_scales = w_quantised[n]
             for g in range(PASSES):
                 nc.tensor.matmul_mx(
-                    out=push_t[:, n, :],
+                    out=push_t[n][:],
                     lhsT=w_codes[:, g, :].bitcast(FP8X4),
                     lhsT_scale=w_scales[:, g, :],
                     rhs=h_codes[:, g, :].bitcast(FP8X4),
@@ -183,31 +194,39 @@ def tile_stackrnncore_pa_s_kernel(tc, h, act_logits, stacks, W_push, b_push, out
                     stop=(g == PASSES - 1),
                 )
 
-        biased_t = keep.tile([P, NS, P], F32)
-        biased = psum.tile([P, NS, CS], F32)
-        for n in range(NS):
+        def turn_back(n):
             nc.scalar.activation(
-                out=biased_t[:, n, :], in_=push_t[:, n, :], func=ACT.Identity, bias=bias_col[:, n : n + 1]
+                out=biased_t[:, n, :], in_=push_t[n][:], func=ACT.Identity, bias=bias_col[:, n : n + 1]
             )
+            nc.tensor.transpose(biased[n][:], biased_t[:, n, :], identity[:])
+
         for n in range(NS):
-            nc.tensor.transpose(biased[:, n, :], biased_t[:, n, :], identity[:])
+            multiply(n)
+        for n in range(NS):
+            turn_back(n)
 
         def top_cell(n):
             nc.vector.scalar_tensor_tensor(
                 out=new[:, n, 0, :],
-                in0=biased[:, n, :],
+                in0=biased[n][:],
                 scalar=act[:, n, 0:1],
                 in1=new[:, n, 0, :],
                 op0=ALU.mult,
                 op1=ALU.add,
             )
 
-        push_term(3, 1, HALF)
-        push_term(3, HALF, SS)
-        pop_term(3, 0, HALF)
-        store(3, 1, HALF)
-        pop_term(3, HALF, SS - 1)
-        store(3, HALF, SS)
+        push_term(3, LATE, SS)
+        store(3, SS - 1, SS)
+        push_term(3, 1, LATE)
+        nc.gpsimd.tensor_tensor(
+            out=new[:, 3, LATE : SS - 1], in0=popped[:], in1=new[:, 3, LATE : SS - 1], op=ALU.add
+        )
         for n in range(NS):
             top_cell(n)
-            store(n, 0, 1)
+            if n < NS - 1:
+                store(n, 0, 1)
+        pop_term(3, 2, LATE)
+        store(3, LATE, SS - 1)
+        store(3, 2, LATE)
+        pop_term(3, 0, 2)
+        store(3, 0, 2)

from contextlib import ExitStack

import concourse.mybir as mybir
from concourse.masks import make_identity

F32 = mybir.dt.float32
BF16 = mybir.dt.bfloat16
U32 = mybir.dt.uint32
U8 = mybir.dt.uint8
FP8X4 = mybir.dt.float8_e4m3fn_x4
ACT = mybir.ActivationFunctionType
ALU = mybir.AluOpType
AX = mybir.AxisListType

P = 128
H = 1024
NS = 4
SS = 8
LATE = 5
HALF = SS // 2
CS = 128
NA = 3
PACK = 4
K_PASS = P * PACK
PASSES = H // K_PASS
PAIRS = 2

FLOPS = 2 * P * H * NS * CS


def tile_stackrnncore_pa_s_kernel(tc, h, act_logits, stacks, W_push, b_push, out):
    nc = tc.nc
    with ExitStack() as ctx:
        keep = ctx.enter_context(tc.tile_pool(name="keep", bufs=1))
        psum = ctx.enter_context(tc.psum_pool(name="psum", bufs=1))
        ctx.enter_context(tc.manual_schedule())

        logits = keep.tile([P, NS * NA], BF16)
        nc.sync.dma_start(out=logits[:], in_=act_logits)

        old = keep.tile([P, NS, SS, CS], BF16)
        h_rows = keep.tile([P, H], BF16)
        w_rows = [keep.tile([P, H], BF16, name="w_rows%d" % n) for n in range(NS)]
        nc.sync.dma_start(out=old[:, 0], in_=stacks[:, 0])
        nc.sync.dma_start(out=old[:, 1], in_=stacks[:, 1])
        nc.sync.dma_start(out=old[:, 2], in_=stacks[:, 2])
        nc.sync.dma_start(out=h_rows[:], in_=h)
        bias_rows = keep.tile([P, CS], BF16)
        nc.gpsimd.memset(bias_rows[:], 0.0)
        nc.sync.dma_start(out=bias_rows[0:NS, :], in_=b_push.rearrange("(n c) -> n c", c=CS))
        for n in range(NS):
            nc.sync.dma_start(out=w_rows[n][:], in_=W_push[n * CS : (n + 1) * CS, :])
        nc.sync.dma_start(out=old[:, 3], in_=stacks[:, 3])

        identity = keep.tile([P, P], F32)
        make_identity(nc, identity[:])
        identity_bf16 = keep.tile([P, P], BF16)
        make_identity(nc, identity_bf16[:])

        zero = keep.tile([P, 1], F32)
        nc.vector.memset(zero[:], 0.0)
        one = keep.tile([P, 1], F32)
        nc.scalar.activation(out=one[:], in_=zero[:], func=ACT.Exp)

        neg_max = keep.tile([P, 1], F32)
        nc.vector.reduce_max(out=neg_max[:], in_=logits[:], axis=AX.X, negate=True)
        expd = keep.tile([P, NS * NA], F32)
        exp_sum = keep.tile([P, 1], F32)
        nc.scalar.activation(
            out=expd[:], in_=logits[:], func=ACT.Exp, bias=neg_max[:], accum_out=exp_sum[:]
        )
        inv_sum = keep.tile([P, 1], F32)
        nc.vector.reciprocal(out=inv_sum[:], in_=exp_sum[:])
        act = keep.tile([P, NS, NA], F32)
        nc.vector.tensor_scalar_mul(
            out=act[:].rearrange("p n a -> p (n a)"), in0=expd[:], scalar1=inv_sum[:]
        )

        new = keep.tile([P, NS, SS, CS], F32)

        nc.vector.tensor_scalar(
            out=new[:, 0, 0:HALF],
            in0=old[:, 0, 0:HALF],
            scalar1=expd[:, 2:3],
            scalar2=inv_sum[:],
            op0=ALU.mult,
            op1=ALU.mult,
        )

        def keep_term(n, first, last):
            nc.scalar.activation(
                out=new[:, n, first:last], in_=old[:, n, first:last], func=ACT.Copy, scale=act[:, n, 2:3]
            )

        def add_term(n, first, last, shift, action):
            nc.vector.scalar_tensor_tensor(
                out=new[:, n, first:last],
                in0=old[:, n, first + shift : last + shift],
                scalar=act[:, n, action : action + 1],
                in1=new[:, n, first:last],
                op0=ALU.mult,
                op1=ALU.add,
            )

        def push_term(n, first, last):
            add_term(n, first, last, -1, 0)

        def pop_term(n, first, last):
            add_term(n, first, last, 1, 1)

        def store(n, first, last):
            nc.sync.dma_start(out=out[:, n, first:last, :], in_=new[:, n, first:last, :])

        def turn(rows, name):
            bank = psum.tile([P, PASSES, PAIRS, P], F32, name="bank_" + name)
            words = rows.bitcast(F32)
            for g in range(PASSES):
                for u in range(PAIRS):
                    first = g * PAIRS * P + u
                    nc.tensor.transpose(
                        bank[:, g, u, :], words[:, first : (g + 1) * PAIRS * P : PAIRS], identity[:]
                    )
            return bank

        def regroup(bank, name):
            grouped = keep.tile([P, PASSES * P * PACK], BF16, align_bytes=64, name="grouped_" + name)
            nc.scalar.copy(
                out=grouped[:].bitcast(F32).rearrange("p (g r u) -> p g r u", g=PASSES, u=PAIRS),
                in_=bank[:].rearrange("p g u r -> p g r u"),
            )
            return grouped

        def quantise(grouped, name):
            codes = keep.tile([P, PASSES, P], U32, align_bytes=64, name="codes_" + name)
            scales = keep.tile([P, PASSES, P], U8, align_bytes=64, name="scales_" + name)
            nc.vector.quantize_mx(
                out=codes[:].rearrange("p g r -> p (g r)").bitcast(FP8X4),
                scales=scales[:].rearrange("p g r -> p (g r)"),
                in_=grouped[:],
            )
            return codes, scales

        h_bank = turn(h_rows[:], "h")
        w_banks = [turn(w_rows[n][:], "w%d" % n) for n in range(NS)]

        bias_bank = psum.tile([P, P], BF16, name="bias_bank")
        nc.tensor.transpose(bias_bank[:], bias_rows[:], identity_bf16[:])

        keep_term(0, HALF, SS)
        keep_term(1, 0, SS)
        keep_term(2, 0, SS)
        h_grouped = regroup(h_bank, "h")
        w_grouped = [regroup(w_banks[n], "w%d" % n) for n in range(NS)]
        keep_term(3, 0, SS)
        popped = keep.tile([P, SS - 1 - LATE, CS], F32)
        nc.scalar.activation(
            out=popped[:], in_=old[:, 3, LATE + 1 : SS], func=ACT.Copy, scale=act[:, 3, 1:2]
        )
        bias_col = keep.tile([P, NS], F32)
        nc.scalar.copy(out=bias_col[:], in_=bias_bank[:, 0:NS])

        push_term(0, 1, HALF)
        push_term(0, HALF, SS)
        pop_term(0, 0, HALF)
        store(0, 1, HALF)
        push_term(1, 1, SS)
        pop_term(0, HALF, SS - 1)
        store(0, HALF, SS)
        push_term(2, 1, SS)
        pop_term(1, 0, SS - 1)
        store(1, 1, SS)
        h_codes, h_scales = quantise(h_grouped, "h")
        w_quantised = [quantise(w_grouped[n], "w%d" % n) for n in range(NS)]
        pop_term(2, 0, SS - 1)
        store(2, 1, SS)

        biased_t = keep.tile([P, NS, P], F32)
        biased = []
        push_t = []
        for n in range(NS):
            push_t.append(psum.tile([P, P], F32, name=("bank_push", "bank_h", "bank_w0", "bank_w1")[n]))
            biased.append(psum.tile([P, CS], F32, name=("bank_top", "bank_w2", "bank_w3", "bias_bank")[n]))

        def multiply(n):
            w_codes, w_scales = w_quantised[n]
            for g in range(PASSES):
                nc.tensor.matmul_mx(
                    out=push_t[n][:],
                    lhsT=w_codes[:, g, :].bitcast(FP8X4),
                    lhsT_scale=w_scales[:, g, :],
                    rhs=h_codes[:, g, :].bitcast(FP8X4),
                    rhs_scale=h_scales[:, g, :],
                    start=(g == 0),
                    stop=(g == PASSES - 1),
                )

        def turn_back(n):
            nc.scalar.activation(
                out=biased_t[:, n, :], in_=push_t[n][:], func=ACT.Identity, bias=bias_col[:, n : n + 1]
            )
            nc.tensor.transpose(biased[n][:], biased_t[:, n, :], identity[:])

        for n in range(NS):
            multiply(n)
        for n in range(NS):
            turn_back(n)

        def top_cell(n):
            nc.vector.scalar_tensor_tensor(
                out=new[:, n, 0, :],
                in0=biased[n][:],
                scalar=act[:, n, 0:1],
                in1=new[:, n, 0, :],
                op0=ALU.mult,
                op1=ALU.add,
            )

        push_term(3, LATE, SS)
        store(3, SS - 1, SS)
        push_term(3, 1, LATE)
        nc.gpsimd.tensor_tensor(
            out=new[:, 3, LATE : SS - 1], in0=popped[:], in1=new[:, 3, LATE : SS - 1], op=ALU.add
        )
        for n in range(NS):
            top_cell(n)
            if n < NS - 1:
                store(n, 0, 1)
        pop_term(3, 2, LATE)
        store(3, LATE, SS - 1)
        store(3, 2, LATE)
        pop_term(3, 0, 2)
        store(3, 0, 2)
